import numpy as np
import ml_dtypes


def mxq(x, axis, fmt="e4m3"):
    dtype, down = {"e4m3": (ml_dtypes.float8_e4m3fn, 7), "e5m2": (ml_dtypes.float8_e5m2, 14)}[fmt]
    v = np.moveaxis(np.asarray(x, np.float32).astype(ml_dtypes.bfloat16).astype(np.float64), axis, -1)
    blocks = v.reshape(v.shape[:-1] + (-1, 32))
    amax = np.abs(blocks).max(-1, keepdims=True)
    byte = np.maximum(np.where(amax > 0, np.frexp(amax)[1] - 1 + 127, 0) - down, 1)
    scale = np.exp2(byte - 127.0)
    codes = (blocks / scale).astype(np.float32).astype(dtype).astype(np.float64)
    return np.moveaxis((codes * scale).reshape(v.shape), -1, axis)


WIDE = False


def mx_kscale(k):
    if not WIDE:
        return np.ones(k)
    levels = np.array([10, -10, 5, -5, 0])
    a = np.random.permutation(np.resize(levels, k // 512 * 4)).reshape(k // 512, 4)
    idx = np.arange(k)
    return np.exp2(a[idx // 512, idx % 128 // 32])


BF16 = ml_dtypes.bfloat16


def bf(x):
    return np.asarray(x, np.float32).astype(BF16)


def f64(x):
    return np.asarray(x).astype(np.float64)


B, LQ, N, LD, D = 16, 256, 2, 1024, 512

EPS = 1e-12


def _l2norm(x):
    n = np.sqrt(np.sum(x * x, axis=-1, keepdims=True))
    return x / np.maximum(n, EPS)


def setup_inputs():
    s = mx_kscale(D)
    c1 = np.exp2(np.round(np.log2(np.sqrt(np.mean(s * s)))))
    c2 = np.exp2(np.round(np.log2(np.sqrt(np.mean(1.0 / (s * s))))))
    x1 = np.random.standard_normal((B, LQ, D)) * s * (np.random.random((B, LQ, 1)) >= 0.0625)
    x2 = np.random.standard_normal((B, N, LD, D)) / s * (np.random.random((B, N, LD, 1)) >= 0.0625)
    x1_mask = (np.random.random((B, LQ)) >= 0.25) * c1
    x2_mask = (np.random.random((B, N, LD)) >= 0.5) * c2
    return {'x1': bf(x1), 'x2': bf(x2), 'x1_mask': bf(x1_mask), 'x2_mask': bf(x2_mask)}


def reference(x1, x2, x1_mask, x2_mask):
    a = _l2norm(f64(x1)) * f64(x1_mask)[..., None]
    d = _l2norm(f64(x2)) * f64(x2_mask)[..., None]
    sim = mxq(a, 2, 'e4m3')[:, None] @ mxq(d, 3, 'e4m3').transpose(0, 1, 3, 2)
    return sim.max(axis=-1).sum(axis=-1)

@@ -1,0 +1,299 @@
+from contextlib import ExitStack
+
+import concourse.mybir as mybir
+from concourse.masks import make_identity
+
+FLOPS = 2 * 16 * 2 * 256 * 1024 * 512
+
+BF16 = mybir.dt.bfloat16
+F32 = mybir.dt.float32
+U32 = mybir.dt.uint32
+U8 = mybir.dt.uint8
+FP8X4 = mybir.dt.float8_e4m3fn_x4
+ALU = mybir.AluOpType
+ACTF = mybir.ActivationFunctionType
+AX = mybir.AxisListType
+
+P = 128
+HALF = 256
+GROUPS = 16
+Q_CHUNKS = 4
+D_CHUNKS = 32
+CHUNKS = Q_CHUNKS + D_CHUNKS
+EPS2 = 1e-24
+
+UNITS = 2 * CHUNKS
+LEAD = 3
+TAIL_UNITS = 4
+
+PINNED = True
+
+
+def tile_lateinteraction_t_kernel(tc, x1, x2, x1_mask, x2_mask, out):
+    nc = tc.nc
+    q_rows = x1.rearrange("b q (u c) -> (b q u) c", u=2)
+    d_rows = x2.rearrange("b n l (u c) -> (b n l u) c", u=2)
+
+    with ExitStack() as ctx:
+        if PINNED:
+            ctx.enter_context(tc.manual_schedule())
+        const = ctx.enter_context(tc.tile_pool(name="const", bufs=1))
+        xpool = ctx.enter_context(tc.tile_pool(name="xpool", bufs=6))
+        small = ctx.enter_context(tc.tile_pool(name="small", bufs=3))
+        work = ctx.enter_context(tc.tile_pool(name="work", bufs=3))
+        ps_t = ctx.enter_context(tc.psum_pool(name="ps_t", bufs=4))
+        ps_m = ctx.enter_context(tc.psum_pool(name="ps_m", bufs=3))
+        ps_q = ctx.enter_context(tc.psum_pool(name="ps_q", bufs=1))
+
+        warm = const.tile([P, 1], F32, name="warm")
+        nc.vector.memset(warm[:], 1.0)
+        nc.scalar.activation(out=warm[:], in_=warm[:], func=ACTF.Sqrt)
+
+        ident = const.tile([P, P], BF16, name="ident")
+        make_identity(nc, ident[:])
+
+        mrow = const.tile([P, 5, 64], BF16, name="mrow")
+        nc.vector.memset(mrow[64:128, 4, :], 0.0)
+        nc.scalar.dma_start(
+            out=mrow[:, 0:4, :],
+            in_=x2_mask.rearrange("b n (g w) -> (b n g) w", w=64).rearrange("(k r) w -> r k w", r=P),
+        )
+        nc.scalar.dma_start(out=mrow[0:64, 4, :], in_=x1_mask.rearrange("b (g w) -> (b g) w", w=64))
+
+        pick = const.tile([P, 4, P], F32, name="pick")
+        nc.vector.memset(pick[:], 0.0)
+        for i in range(4):
+            nc.vector.memset(pick[:, i, i : i + 1], 1.0)
+        rsum = const.tile([P, 64], F32, name="rsum")
+        nc.vector.tensor_reduce(
+            out=rsum[:], in_=ident[:].rearrange("p (w u) -> p w u", u=2), axis=AX.X, op=ALU.add
+        )
+        pairm = const.tile([P, 64, 2], F32, name="pairm")
+        nc.vector.tensor_copy(out=pairm[:], in_=rsum[:].unsqueeze(2).to_broadcast([P, 64, 2]))
+
+        mdup = const.tile([P, 5, 64, 2], BF16, name="mdup")
+        nc.vector.tensor_copy(out=mdup[:], in_=mrow[:].unsqueeze(3).to_broadcast([P, 5, 64, 2]))
+        pmk = ps_q.tile([P, 5, P], BF16, name="pmk", tag="pq")
+        for k in range(5):
+            nc.tensor.transpose(
+                out=pmk[:, k, :], in_=mdup[:, k, :, :].rearrange("p w u -> p (w u)"), identity=ident[:]
+            )
+        mask_t = const.tile([P, 5 * P], F32, name="mask_t")
+        nc.vector.tensor_copy(out=mask_t[:], in_=pmk[:].rearrange("p k r -> p (k r)"))
+
+        junk = const.tile([P, HALF], BF16, name="junk")
+        a_cod = const.tile([P, Q_CHUNKS * 1024], U32, name="a_cod", align_bytes=64)
+        a_scl = const.tile([P, Q_CHUNKS * 1024], U8, name="a_scl", align_bytes=64)
+        best = const.tile([P, D_CHUNKS * 4], F32, name="best")
+
+        xr_t = {}
+        ss_t = {}
+        sq_t = {}
+        sc_t = {}
+        xs_t = {}
+        pt_t = {}
+        grp_t = {}
+        cod_t = {}
+        pm_t = {}
+
+        def ok(c):
+            return 0 <= c < CHUNKS
+
+        def load(c):
+            if not ok(c):
+                return
+            rows = q_rows[c * 2048 : (c + 1) * 2048, :] if c < Q_CHUNKS else d_rows[(c - Q_CHUNKS) * 2048 : (c - Q_CHUNKS + 1) * 2048, :]
+            xr = xpool.tile([P, GROUPS, HALF], BF16, name="xr", tag="xr")
+            xr_t[c] = xr
+            pieces = 4 if c == 0 else (2 if c == 1 else 1)
+            step = GROUPS // pieces
+            for i in range(pieces):
+                nc.sync.dma_start(
+                    out=xr[:, i * step : (i + 1) * step, :],
+                    in_=rows[i * step * P : (i + 1) * step * P, :].rearrange("(g p) c -> p g c", p=P),
+                )
+
+        def sumsq(c, g0, g1):
+            if not ok(c):
+                return
+            if g0 == 0:
+                ss = small.tile([P, GROUPS], F32, name="ss", tag="ss")
+                ss_t[c] = ss
+            for g in range(g0, g1):
+                nc.scalar.activation(
+                    out=junk[:], in_=xr_t[c][:, g, :], func=ACTF.Square, accum_out=ss_t[c][:, g : g + 1]
+                )
+
+        def pair_sum(c):
+            if not ok(c):
+                return
+            pq = ps_q.tile([P, GROUPS], F32, name="pq", tag="pq")
+            nc.tensor.matmul(
+                out=pq[:], lhsT=pairm[:].rearrange("p w u -> p (w u)"), rhs=ss_t[c][:], start=True, stop=True
+            )
+            pt_t[("pq", c)] = pq
+
+        def clamp(c):
+            if not ok(c):
+                return
+            cl = small.tile([P, GROUPS], F32, name="cl", tag="cl")
+            nc.vector.tensor_scalar_max(out=cl[:], in0=pt_t[("pq", c)][:], scalar1=EPS2)
+            sq_t[c] = cl
+
+        def root(c):
+            if not ok(c):
+                return
+            rt = small.tile([P, GROUPS], F32, name="rt", tag="rt")
+            nc.scalar.activation(out=rt[:], in_=sq_t[c][:], func=ACTF.Sqrt)
+            sq_t[c] = rt
+
+        def factor(c):
+            if not ok(c):
+                return
+            rc = small.tile([P, GROUPS], F32, name="rc", tag="rc")
+            nc.vector.reciprocal(out=rc[:], in_=sq_t[c][:])
+            sc = small.tile([P, GROUPS], F32, name="sc", tag="sc")
+            col = 512 + c * GROUPS if c < Q_CHUNKS else (c - Q_CHUNKS) * GROUPS
+            nc.vector.tensor_tensor(out=sc[:], in0=rc[:], in1=mask_t[:, col : col + GROUPS], op=ALU.mult)
+            sc_t[c] = sc
+
+        def scale_and_turn(c, h):
+            if not ok(c):
+                return
+            xs = work.tile([P, 8, HALF], BF16, name="xs", tag="xs")
+            for bank in range(2):
+                for gl in range(4):
+                    g = h * 8 + bank * 4 + gl
+                    nc.vector.tensor_scalar(
+                        out=xs[:, bank * 4 + gl, :],
+                        in0=xr_t[c][:, g, :],
+                        scalar1=sc_t[c][:, g : g + 1],
+                        scalar2=None,
+                        op0=ALU.mult,
+                    )
+                pt = ps_t.tile([P, 4, 64, 2, 2], BF16, name="pt", tag="pt")
+                pt_t[(c, h, bank)] = pt
+                for gl in range(4):
+                    for v in range(2):
+                        nc.tensor.transpose(
+                            out=pt[:, gl, :, v, :],
+                            in_=xs[:, bank * 4 + gl, v * P : (v + 1) * P],
+                            identity=ident[:],
+                        )
+
+        def leave(u, bank, on_scalar):
+            c, h = unit(u)
+            if bank == 0:
+                grp = work.tile([P, 2048], BF16, name="grp", tag="grp", align_bytes=64)
+                grp_t[(c, h)] = grp
+            src = pt_t[(c, h, bank)][:].rearrange("p a w v u -> p (a w v u)")
+            dst = grp_t[(c, h)][:, bank * 1024 : (bank + 1) * 1024]
+            if on_scalar:
+                nc.scalar.copy(out=dst, in_=src)
+            else:
+                nc.vector.tensor_copy(out=dst, in_=src)
+
+        def quantise(c, h):
+            if not ok(c):
+                return
+            if c < Q_CHUNKS:
+                lo = c * 1024 + h * 512
+                cod = a_cod[:, lo : lo + 512]
+                scl = a_scl[:, lo : lo + 512]
+            else:
+                cod_tile = work.tile([P, 512], U32, name="cod_tile", tag="cod", align_bytes=64)
+                scl_tile = work.tile([P, 512], U8, name="scl_tile", tag="scl", align_bytes=64)
+                cod = cod_tile[:]
+                scl = scl_tile[:]
+                cod_t[(c, h)] = (cod, scl)
+            nc.vector.quantize_mx(out=cod.bitcast(FP8X4), scales=scl, in_=grp_t[(c, h)][:])
+
+        def multiply(c, h):
+            if not ok(c) or c < Q_CHUNKS:
+                return
+            d = c - Q_CHUNKS
+            b = d // 2
+            cod, scl = cod_t[(c, h)]
+            for qt in range(2):
+                lo = b * 256 + qt * P
+                pm = ps_m.tile([P, 512], F32, name="pm", tag="pm")
+                pm_t[(c, h, qt)] = pm
+                nc.tensor.matmul_mx(
+                    out=pm[:],
+                    lhsT=a_cod[:, lo : lo + P].bitcast(FP8X4),
+                    lhsT_scale=a_scl[:, lo : lo + P],
+                    rhs=cod.bitcast(FP8X4),
+                    rhs_scale=scl,
+                    start=True,
+                    stop=True,
+                )
+
+        def best_of(u, qt):
+            c, h = unit(u)
+            if c < Q_CHUNKS:
+                return
+            col = (c - Q_CHUNKS) * 4 + qt * 2 + h
+            nc.vector.tensor_reduce(
+                out=best[:, col : col + 1], in_=pm_t[(c, h, qt)][:], axis=AX.X, op=ALU.max
+            )
+
+        def unit(u):
+            return u // 2, u % 2
+
+        def act_banks(u):
+            if u < 2 * Q_CHUNKS:
+                return 0
+            if u >= UNITS - TAIL_UNITS:
+                return 2
+            return 1
+
+        for c in range(LEAD):
+            load(c)
+        for s in range(UNITS + 6):
+            if s % 2 == 0:
+                load(s // 2 + LEAD)
+            j = s // 2 - 1
+            chain = s % 2 == 0
+            if 0 <= s - 5 < UNITS:
+                quantise(*unit(s - 5))
+            if chain:
+                pair_sum(j)
+            if 0 <= s - 5 < UNITS:
+                multiply(*unit(s - 5))
+            if s < UNITS:
+                sumsq(s // 2, (s % 2) * 8, (s % 2) * 8 + 4)
+            if 0 <= s - 3 < UNITS:
+                scale_and_turn(*unit(s - 3))
+            if chain:
+                clamp(j)
+            if 0 <= s - 4 < UNITS:
+                leave(s - 4, 0, act_banks(s - 4) >= 1)
+            if chain:
+                root(j)
+            if 0 <= s - 4 < UNITS:
+                leave(s - 4, 1, act_banks(s - 4) >= 2)
+            if s < UNITS:
+                sumsq(s // 2, (s % 2) * 8 + 4, (s % 2) * 8 + 8)
+            if 0 <= s - 5 < UNITS:
+                best_of(s - 5, 0)
+            if chain:
+                factor(j)
+            if 0 <= s - 5 < UNITS:
+                best_of(s - 5, 1)
+
+        both = const.tile([P, D_CHUNKS * 2], F32, name="both")
+        nc.vector.tensor_reduce(
+            out=both[:], in_=best[:].rearrange("p (a h) -> p a h", h=2), axis=AX.X, op=ALU.max
+        )
+        tot = const.tile([P, D_CHUNKS], F32, name="tot")
+        nc.vector.tensor_reduce(
+            out=tot[:], in_=both[:].rearrange("p (d q) -> p d q", q=2), axis=AX.X, op=ALU.add
+        )
+        pf = ps_q.tile([P, 8], F32, name="pf", tag="pq")
+        for i in range(4):
+            nc.tensor.matmul(
+                out=pf[:], lhsT=pick[:, i, :], rhs=tot[:, i * 8 : (i + 1) * 8], start=(i == 0), stop=(i == 3)
+            )
+        res = const.tile([P, 8], F32, name="res")
+        nc.vector.tensor_copy(out=res[:], in_=pf[:])
+        nc.sync.dma_start(out=out.rearrange("(i b) n -> i (b n)", i=4), in_=res[0:4, :])

@@ -27,6 +27,7 @@ LEAD = 3
 TAIL_UNITS = 4
 
 PINNED = True
+HEAT = True
 
 
 def tile_lateinteraction_t_kernel(tc, x1, x2, x1_mask, x2_mask, out):
@@ -42,7 +43,8 @@ def tile_lateinteraction_t_kernel(tc, x1, x2, x1_mask, x2_mask, out):
         small = ctx.enter_context(tc.tile_pool(name="small", bufs=3))
         work = ctx.enter_context(tc.tile_pool(name="work", bufs=3))
         ps_t = ctx.enter_context(tc.psum_pool(name="ps_t", bufs=4))
-        ps_m = ctx.enter_context(tc.psum_pool(name="ps_m", bufs=3))
+        ps_m = ctx.enter_context(tc.psum_pool(name="ps_m", bufs=2))
+        ps_f = ctx.enter_context(tc.psum_pool(name="ps_f", bufs=1))
         ps_q = ctx.enter_context(tc.psum_pool(name="ps_q", bufs=1))
 
         warm = const.tile([P, 1], F32, name="warm")
@@ -81,6 +83,7 @@ def tile_lateinteraction_t_kernel(tc, x1, x2, x1_mask, x2_mask, out):
         mask_t = const.tile([P, 5 * P], F32, name="mask_t")
         nc.vector.tensor_copy(out=mask_t[:], in_=pmk[:].rearrange("p k r -> p (k r)"))
 
+        heat = ps_f.tile([P, P], F32, name="heat")
         junk = const.tile([P, HALF], BF16, name="junk")
         a_cod = const.tile([P, Q_CHUNKS * 1024], U32, name="a_cod", align_bytes=64)
         a_scl = const.tile([P, Q_CHUNKS * 1024], U8, name="a_scl", align_bytes=64)
@@ -180,6 +183,14 @@ def tile_lateinteraction_t_kernel(tc, x1, x2, x1_mask, x2_mask, out):
                             in_=xs[:, bank * 4 + gl, v * P : (v + 1) * P],
                             identity=ident[:],
                         )
+                if HEAT:
+                    nc.tensor.matmul(
+                        out=heat[:],
+                        lhsT=pairm[:].rearrange("p w u -> p (w u)"),
+                        rhs=mask_t[:, 0:P],
+                        start=True,
+                        stop=True,
+                    )
 
         def leave(u, bank, on_scalar):
             c, h = unit(u)

@@ -27,7 +27,6 @@ LEAD = 3
 TAIL_UNITS = 4
 
 PINNED = True
-HEAT = True
 
 
 def tile_lateinteraction_t_kernel(tc, x1, x2, x1_mask, x2_mask, out):
@@ -43,8 +42,7 @@ def tile_lateinteraction_t_kernel(tc, x1, x2, x1_mask, x2_mask, out):
         small = ctx.enter_context(tc.tile_pool(name="small", bufs=3))
         work = ctx.enter_context(tc.tile_pool(name="work", bufs=3))
         ps_t = ctx.enter_context(tc.psum_pool(name="ps_t", bufs=4))
-        ps_m = ctx.enter_context(tc.psum_pool(name="ps_m", bufs=2))
-        ps_f = ctx.enter_context(tc.psum_pool(name="ps_f", bufs=1))
+        ps_m = ctx.enter_context(tc.psum_pool(name="ps_m", bufs=3))
         ps_q = ctx.enter_context(tc.psum_pool(name="ps_q", bufs=1))
 
         warm = const.tile([P, 1], F32, name="warm")
@@ -83,8 +81,7 @@ def tile_lateinteraction_t_kernel(tc, x1, x2, x1_mask, x2_mask, out):
         mask_t = const.tile([P, 5 * P], F32, name="mask_t")
         nc.vector.tensor_copy(out=mask_t[:], in_=pmk[:].rearrange("p k r -> p (k r)"))
 
-        heat = ps_f.tile([P, P], F32, name="heat")
-        junk = const.tile([P, HALF], BF16, name="junk")
+        junk = const.tile([P, 8, HALF], BF16, name="junk")
         a_cod = const.tile([P, Q_CHUNKS * 1024], U32, name="a_cod", align_bytes=64)
         a_scl = const.tile([P, Q_CHUNKS * 1024], U8, name="a_scl", align_bytes=64)
         best = const.tile([P, D_CHUNKS * 4], F32, name="best")
@@ -124,7 +121,7 @@ def tile_lateinteraction_t_kernel(tc, x1, x2, x1_mask, x2_mask, out):
                 ss_t[c] = ss
             for g in range(g0, g1):
                 nc.scalar.activation(
-                    out=junk[:], in_=xr_t[c][:, g, :], func=ACTF.Square, accum_out=ss_t[c][:, g : g + 1]
+                    out=junk[:, g % 8, :], in_=xr_t[c][:, g, :], func=ACTF.Square, accum_out=ss_t[c][:, g : g + 1]
                 )
 
         def pair_sum(c):
@@ -183,14 +180,6 @@ def tile_lateinteraction_t_kernel(tc, x1, x2, x1_mask, x2_mask, out):
                             in_=xs[:, bank * 4 + gl, v * P : (v + 1) * P],
                             identity=ident[:],
                         )
-                if HEAT:
-                    nc.tensor.matmul(
-                        out=heat[:],
-                        lhsT=pairm[:].rearrange("p w u -> p (w u)"),
-                        rhs=mask_t[:, 0:P],
-                        start=True,
-                        stop=True,
-                    )
 
         def leave(u, bank, on_scalar):
             c, h = unit(u)

@@ -147,14 +147,19 @@ def tile_lateinteraction_t_kernel(tc, x1, x2, x1_mask, x2_mask, out):
             nc.scalar.activation(out=rt[:], in_=sq_t[c][:], func=ACTF.Sqrt)
             sq_t[c] = rt
 
-        def factor(c):
+        def invert(c):
             if not ok(c):
                 return
             rc = small.tile([P, GROUPS], F32, name="rc", tag="rc")
             nc.vector.reciprocal(out=rc[:], in_=sq_t[c][:])
+            sq_t[c] = rc
+
+        def factor(c):
+            if not ok(c):
+                return
             sc = small.tile([P, GROUPS], F32, name="sc", tag="sc")
             col = 512 + c * GROUPS if c < Q_CHUNKS else (c - Q_CHUNKS) * GROUPS
-            nc.vector.tensor_tensor(out=sc[:], in0=rc[:], in1=mask_t[:, col : col + GROUPS], op=ALU.mult)
+            nc.vector.tensor_tensor(out=sc[:], in0=sq_t[c][:], in1=mask_t[:, col : col + GROUPS], op=ALU.mult)
             sc_t[c] = sc
 
         def scale_and_turn(c, h):
@@ -277,9 +282,11 @@ def tile_lateinteraction_t_kernel(tc, x1, x2, x1_mask, x2_mask, out):
             if 0 <= s - 5 < UNITS:
                 best_of(s - 5, 0)
             if chain:
-                factor(j)
+                invert(j)
             if 0 <= s - 5 < UNITS:
                 best_of(s - 5, 1)
+            if chain:
+                factor(j)
 
         both = const.tile([P, D_CHUNKS * 2], F32, name="both")
         nc.vector.tensor_reduce(

@@ -15,8 +15,8 @@ ACTF = mybir.ActivationFunctionType
 AX = mybir.AxisListType
 
 P = 128
-HALF = 256
-GROUPS = 16
+D = 512
+GROUPS = 8
 Q_CHUNKS = 4
 D_CHUNKS = 32
 CHUNKS = Q_CHUNKS + D_CHUNKS
@@ -26,17 +26,12 @@ UNITS = 2 * CHUNKS
 LEAD = 3
 TAIL_UNITS = 4
 
-PINNED = True
-
 
 def tile_lateinteraction_t_kernel(tc, x1, x2, x1_mask, x2_mask, out):
     nc = tc.nc
-    q_rows = x1.rearrange("b q (u c) -> (b q u) c", u=2)
-    d_rows = x2.rearrange("b n l (u c) -> (b n l u) c", u=2)
 
     with ExitStack() as ctx:
-        if PINNED:
-            ctx.enter_context(tc.manual_schedule())
+        ctx.enter_context(tc.manual_schedule())
         const = ctx.enter_context(tc.tile_pool(name="const", bufs=1))
         xpool = ctx.enter_context(tc.tile_pool(name="xpool", bufs=6))
         small = ctx.enter_context(tc.tile_pool(name="small", bufs=3))
@@ -49,39 +44,25 @@ def tile_lateinteraction_t_kernel(tc, x1, x2, x1_mask, x2_mask, out):
         nc.vector.memset(warm[:], 1.0)
         nc.scalar.activation(out=warm[:], in_=warm[:], func=ACTF.Sqrt)
 
-        ident = const.tile([P, P], BF16, name="ident")
+        ident = const.tile([P, P], F32, name="ident")
         make_identity(nc, ident[:])
 
-        mrow = const.tile([P, 5, 64], BF16, name="mrow")
-        nc.vector.memset(mrow[64:128, 4, :], 0.0)
+        mask_t = const.tile([P, CHUNKS * GROUPS], BF16, name="mask_t")
         nc.scalar.dma_start(
-            out=mrow[:, 0:4, :],
-            in_=x2_mask.rearrange("b n (g w) -> (b n g) w", w=64).rearrange("(k r) w -> r k w", r=P),
+            out=mask_t[:, 0 : Q_CHUNKS * GROUPS].rearrange("p (b j) -> p b j", j=2),
+            in_=x1_mask.rearrange("b (p j) -> p b j", j=2),
         )
-        nc.scalar.dma_start(out=mrow[0:64, 4, :], in_=x1_mask.rearrange("b (g w) -> (b g) w", w=64))
+        nc.scalar.dma_start(
+            out=mask_t[:, Q_CHUNKS * GROUPS :].rearrange("p (d j) -> p d j", j=GROUPS),
+            in_=x2_mask.rearrange("b n (p j) -> p (b n) j", j=GROUPS),
+        )
 
         pick = const.tile([P, 4, P], F32, name="pick")
         nc.vector.memset(pick[:], 0.0)
         for i in range(4):
             nc.vector.memset(pick[:, i, i : i + 1], 1.0)
-        rsum = const.tile([P, 64], F32, name="rsum")
-        nc.vector.tensor_reduce(
-            out=rsum[:], in_=ident[:].rearrange("p (w u) -> p w u", u=2), axis=AX.X, op=ALU.add
-        )
-        pairm = const.tile([P, 64, 2], F32, name="pairm")
-        nc.vector.tensor_copy(out=pairm[:], in_=rsum[:].unsqueeze(2).to_broadcast([P, 64, 2]))
 
-        mdup = const.tile([P, 5, 64, 2], BF16, name="mdup")
-        nc.vector.tensor_copy(out=mdup[:], in_=mrow[:].unsqueeze(3).to_broadcast([P, 5, 64, 2]))
-        pmk = ps_q.tile([P, 5, P], BF16, name="pmk", tag="pq")
-        for k in range(5):
-            nc.tensor.transpose(
-                out=pmk[:, k, :], in_=mdup[:, k, :, :].rearrange("p w u -> p (w u)"), identity=ident[:]
-            )
-        mask_t = const.tile([P, 5 * P], F32, name="mask_t")
-        nc.vector.tensor_copy(out=mask_t[:], in_=pmk[:].rearrange("p k r -> p (k r)"))
-
-        junk = const.tile([P, 8, HALF], BF16, name="junk")
+        junk = const.tile([P, 8, D], BF16, name="junk")
         a_cod = const.tile([P, Q_CHUNKS * 1024], U32, name="a_cod", align_bytes=64)
         a_scl = const.tile([P, Q_CHUNKS * 1024], U8, name="a_scl", align_bytes=64)
         best = const.tile([P, D_CHUNKS * 4], F32, name="best")
@@ -90,7 +71,6 @@ def tile_lateinteraction_t_kernel(tc, x1, x2, x1_mask, x2_mask, out):
         ss_t = {}
         sq_t = {}
         sc_t = {}
-        xs_t = {}
         pt_t = {}
         grp_t = {}
         cod_t = {}
@@ -102,15 +82,21 @@ def tile_lateinteraction_t_kernel(tc, x1, x2, x1_mask, x2_mask, out):
         def load(c):
             if not ok(c):
                 return
-            rows = q_rows[c * 2048 : (c + 1) * 2048, :] if c < Q_CHUNKS else d_rows[(c - Q_CHUNKS) * 2048 : (c - Q_CHUNKS + 1) * 2048, :]
-            xr = xpool.tile([P, GROUPS, HALF], BF16, name="xr", tag="xr")
+            xr = xpool.tile([P, GROUPS, D], BF16, name="xr", tag="xr")
             xr_t[c] = xr
-            pieces = 4 if c == 0 else (2 if c == 1 else 1)
-            step = GROUPS // pieces
-            for i in range(pieces):
+            if c < Q_CHUNKS:
+                pieces = 4 if c == 0 else (2 if c == 1 else 1)
+                step = 4 // pieces
+                for i in range(pieces):
+                    nc.sync.dma_start(
+                        out=xr[:, i * step * 2 : (i + 1) * step * 2, :].rearrange("p (b j) k -> p b (j k)", j=2),
+                        in_=x1[c * 4 + i * step : c * 4 + (i + 1) * step].rearrange("b (p j) k -> p b (j k)", j=2),
+                    )
+            else:
+                d = c - Q_CHUNKS
                 nc.sync.dma_start(
-                    out=xr[:, i * step : (i + 1) * step, :],
-                    in_=rows[i * step * P : (i + 1) * step * P, :].rearrange("(g p) c -> p g c", p=P),
+                    out=xr[:].rearrange("p j k -> p (j k)"),
+                    in_=x2[d // 2, d % 2].rearrange("(p j) k -> p (j k)", j=GROUPS),
                 )
 
         def sumsq(c, g0, g1):
@@ -121,23 +107,14 @@ def tile_lateinteraction_t_kernel(tc, x1, x2, x1_mask, x2_mask, out):
                 ss_t[c] = ss
             for g in range(g0, g1):
                 nc.scalar.activation(
-                    out=junk[:, g % 8, :], in_=xr_t[c][:, g, :], func=ACTF.Square, accum_out=ss_t[c][:, g : g + 1]
+                    out=junk[:, g, :], in_=xr_t[c][:, g, :], func=ACTF.Square, accum_out=ss_t[c][:, g : g + 1]
                 )
-
-        def pair_sum(c):
-            if not ok(c):
-                return
-            pq = ps_q.tile([P, GROUPS], F32, name="pq", tag="pq")
-            nc.tensor.matmul(
-                out=pq[:], lhsT=pairm[:].rearrange("p w u -> p (w u)"), rhs=ss_t[c][:], start=True, stop=True
-            )
-            pt_t[("pq", c)] = pq
 
         def clamp(c):
             if not ok(c):
                 return
             cl = small.tile([P, GROUPS], F32, name="cl", tag="cl")
-            nc.vector.tensor_scalar_max(out=cl[:], in0=pt_t[("pq", c)][:], scalar1=EPS2)
+            nc.vector.tensor_scalar_max(out=cl[:], in0=ss_t[c][:], scalar1=EPS2)
             sq_t[c] = cl
 
         def root(c):
@@ -158,41 +135,39 @@ def tile_lateinteraction_t_kernel(tc, x1, x2, x1_mask, x2_mask, out):
             if not ok(c):
                 return
             sc = small.tile([P, GROUPS], F32, name="sc", tag="sc")
-            col = 512 + c * GROUPS if c < Q_CHUNKS else (c - Q_CHUNKS) * GROUPS
-            nc.vector.tensor_tensor(out=sc[:], in0=sq_t[c][:], in1=mask_t[:, col : col + GROUPS], op=ALU.mult)
+            nc.vector.tensor_tensor(
+                out=sc[:], in0=sq_t[c][:], in1=mask_t[:, c * GROUPS : (c + 1) * GROUPS], op=ALU.mult
+            )
             sc_t[c] = sc
 
         def scale_and_turn(c, h):
             if not ok(c):
                 return
-            xs = work.tile([P, 8, HALF], BF16, name="xs", tag="xs")
+            xs = work.tile([P, 4, D], BF16, name="xs", tag="xs")
             for bank in range(2):
-                for gl in range(4):
-                    g = h * 8 + bank * 4 + gl
+                for gl in range(2):
+                    g = h * 4 + bank * 2 + gl
                     nc.vector.tensor_scalar(
-                        out=xs[:, bank * 4 + gl, :],
+                        out=xs[:, bank * 2 + gl, :],
                         in0=xr_t[c][:, g, :],
                         scalar1=sc_t[c][:, g : g + 1],
                         scalar2=None,
                         op0=ALU.mult,
                     )
-                pt = ps_t.tile([P, 4, 64, 2, 2], BF16, name="pt", tag="pt")
+                pt = ps_t.tile([P, 2, 2, P], F32, name="pt", tag="pt")
                 pt_t[(c, h, bank)] = pt
-                for gl in range(4):
-                    for v in range(2):
-                        nc.tensor.transpose(
-                            out=pt[:, gl, :, v, :],
-                            in_=xs[:, bank * 4 + gl, v * P : (v + 1) * P],
-                            identity=ident[:],
-                        )
+                for gl in range(2):
+                    words = xs[:, bank * 2 + gl, :].bitcast(F32)
+                    for u in range(2):
+                        nc.tensor.transpose(out=pt[:, gl, u, :], in_=words[:, u * P : (u + 1) * P], identity=ident[:])
 
         def leave(u, bank, on_scalar):
             c, h = unit(u)
             if bank == 0:
                 grp = work.tile([P, 2048], BF16, name="grp", tag="grp", align_bytes=64)
                 grp_t[(c, h)] = grp
-            src = pt_t[(c, h, bank)][:].rearrange("p a w v u -> p (a w v u)")
-            dst = grp_t[(c, h)][:, bank * 1024 : (bank + 1) * 1024]
+            src = pt_t[(c, h, bank)][:].rearrange("p j u r -> p j r u")
+            dst = grp_t[(c, h)][:, bank * 1024 : (bank + 1) * 1024].bitcast(F32).rearrange("p (j r u) -> p j r u", j=2, u=2)
             if on_scalar:
                 nc.scalar.copy(out=dst, in_=src)
             else:
@@ -261,12 +236,10 @@ def tile_lateinteraction_t_kernel(tc, x1, x2, x1_mask, x2_mask, out):
             chain = s % 2 == 0
             if 0 <= s - 5 < UNITS:
                 quantise(*unit(s - 5))
-            if chain:
-                pair_sum(j)
             if 0 <= s - 5 < UNITS:
                 multiply(*unit(s - 5))
             if s < UNITS:
-                sumsq(s // 2, (s % 2) * 8, (s % 2) * 8 + 4)
+                sumsq(s // 2, (s % 2) * 4, (s % 2) * 4 + 2)
             if 0 <= s - 3 < UNITS:
                 scale_and_turn(*unit(s - 3))
             if chain:
@@ -278,7 +251,7 @@ def tile_lateinteraction_t_kernel(tc, x1, x2, x1_mask, x2_mask, out):
             if 0 <= s - 4 < UNITS:
                 leave(s - 4, 1, act_banks(s - 4) >= 2)
             if s < UNITS:
-                sumsq(s // 2, (s % 2) * 8 + 4, (s % 2) * 8 + 8)
+                sumsq(s // 2, (s % 2) * 4 + 2, (s % 2) * 4 + 4)
             if 0 <= s - 5 < UNITS:
                 best_of(s - 5, 0)
             if chain:

@@ -25,6 +25,7 @@ EPS2 = 1e-24
 UNITS = 2 * CHUNKS
 LEAD = 3
 TAIL_UNITS = 4
+POOL_GROUPS = 2
 
 
 def tile_lateinteraction_t_kernel(tc, x1, x2, x1_mask, x2_mask, out):
@@ -34,7 +35,7 @@ def tile_lateinteraction_t_kernel(tc, x1, x2, x1_mask, x2_mask, out):
         ctx.enter_context(tc.manual_schedule())
         const = ctx.enter_context(tc.tile_pool(name="const", bufs=1))
         xpool = ctx.enter_context(tc.tile_pool(name="xpool", bufs=6))
-        small = ctx.enter_context(tc.tile_pool(name="small", bufs=3))
+        small = ctx.enter_context(tc.tile_pool(name="small", bufs=4))
         work = ctx.enter_context(tc.tile_pool(name="work", bufs=3))
         ps_t = ctx.enter_context(tc.psum_pool(name="ps_t", bufs=4))
         ps_m = ctx.enter_context(tc.psum_pool(name="ps_m", bufs=3))
@@ -47,15 +48,19 @@ def tile_lateinteraction_t_kernel(tc, x1, x2, x1_mask, x2_mask, out):
         ident = const.tile([P, P], F32, name="ident")
         make_identity(nc, ident[:])
 
-        mask_t = const.tile([P, CHUNKS * GROUPS], BF16, name="mask_t")
+        QCOLS = Q_CHUNKS * GROUPS
+        mask_q = const.tile([P, QCOLS], BF16, name="mask_q")
+        mask_d = const.tile([P, D_CHUNKS * GROUPS], BF16, name="mask_d")
         nc.scalar.dma_start(
-            out=mask_t[:, 0 : Q_CHUNKS * GROUPS].rearrange("p (b j) -> p b j", j=2),
+            out=mask_q[:].rearrange("p (b j) -> p b j", j=2),
             in_=x1_mask.rearrange("b (p j) -> p b j", j=2),
         )
         nc.scalar.dma_start(
-            out=mask_t[:, Q_CHUNKS * GROUPS :].rearrange("p (d j) -> p d j", j=GROUPS),
+            out=mask_d[:].rearrange("p (d j) -> p d j", j=GROUPS),
             in_=x2_mask.rearrange("b n (p j) -> p (b n) j", j=GROUPS),
         )
+        mask_f = const.tile([P, CHUNKS * GROUPS], F32, name="mask_f")
+        nc.gpsimd.tensor_copy(out=mask_f[:, 0:QCOLS], in_=mask_q[:])
 
         pick = const.tile([P, 4, P], F32, name="pick")
         nc.vector.memset(pick[:], 0.0)
@@ -70,17 +75,17 @@ def tile_lateinteraction_t_kernel(tc, x1, x2, x1_mask, x2_mask, out):
         xr_t = {}
         ss_t = {}
         sq_t = {}
-        sc_t = {}
+        xs_t = {}
         pt_t = {}
         grp_t = {}
         cod_t = {}
         pm_t = {}
 
-        def ok(c):
-            return 0 <= c < CHUNKS
+        def ok(u):
+            return 0 <= u < UNITS
 
         def load(c):
-            if not ok(c):
+            if not 0 <= c < CHUNKS:
                 return
             xr = xpool.tile([P, GROUPS, D], BF16, name="xr", tag="xr")
             xr_t[c] = xr
@@ -99,105 +104,108 @@ def tile_lateinteraction_t_kernel(tc, x1, x2, x1_mask, x2_mask, out):
                     in_=x2[d // 2, d % 2].rearrange("(p j) k -> p (j k)", j=GROUPS),
                 )
 
-        def sumsq(c, g0, g1):
-            if not ok(c):
+        def sumsq(u, k0, k1):
+            if not ok(u):
                 return
-            if g0 == 0:
-                ss = small.tile([P, GROUPS], F32, name="ss", tag="ss")
-                ss_t[c] = ss
-            for g in range(g0, g1):
+            if k0 == 0:
+                ss = small.tile([P, 4], F32, name="ss", tag="ss")
+                ss_t[u] = ss
+            for k in range(k0, k1):
+                g = (u % 2) * 4 + k
                 nc.scalar.activation(
-                    out=junk[:, g, :], in_=xr_t[c][:, g, :], func=ACTF.Square, accum_out=ss_t[c][:, g : g + 1]
+                    out=junk[:, g, :], in_=xr_t[u // 2][:, g, :], func=ACTF.Square, accum_out=ss_t[u][:, k : k + 1]
                 )
 
-        def clamp(c):
-            if not ok(c):
+        def clamp(u):
+            if not ok(u):
                 return
-            cl = small.tile([P, GROUPS], F32, name="cl", tag="cl")
-            nc.vector.tensor_scalar_max(out=cl[:], in0=ss_t[c][:], scalar1=EPS2)
-            sq_t[c] = cl
+            cl = small.tile([P, 4], F32, name="cl", tag="cl")
+            nc.gpsimd.tensor_scalar(out=cl[:], in0=ss_t[u][:], scalar1=EPS2, scalar2=0.0, op0=ALU.max, op1=ALU.add)
+            sq_t[u] = cl
 
-        def root(c):
-            if not ok(c):
+        def root(u):
+            if not ok(u):
                 return
-            rt = small.tile([P, GROUPS], F32, name="rt", tag="rt")
-            nc.scalar.activation(out=rt[:], in_=sq_t[c][:], func=ACTF.Sqrt)
-            sq_t[c] = rt
+            rt = small.tile([P, 4], F32, name="rt", tag="rt")
+            nc.scalar.activation(out=rt[:], in_=sq_t[u][:], func=ACTF.Sqrt)
+            sq_t[u] = rt
 
-        def invert(c):
-            if not ok(c):
+        def invert(u):
+            if not ok(u):
                 return
-            rc = small.tile([P, GROUPS], F32, name="rc", tag="rc")
-            nc.vector.reciprocal(out=rc[:], in_=sq_t[c][:])
-            sq_t[c] = rc
+            rc = small.tile([P, 4], F32, name="rc", tag="rc")
+            nc.vector.reciprocal(out=rc[:], in_=sq_t[u][:])
+            sq_t[u] = rc
 
-        def factor(c):
-            if not ok(c):
+        def scale(u, on_pool):
+            if not ok(u):
                 return
-            sc = small.tile([P, GROUPS], F32, name="sc", tag="sc")
-            nc.vector.tensor_tensor(
-                out=sc[:], in0=sq_t[c][:], in1=mask_t[:, c * GROUPS : (c + 1) * GROUPS], op=ALU.mult
-            )
-            sc_t[c] = sc
+            ks = range(0, POOL_GROUPS) if on_pool else range(POOL_GROUPS, 4)
+            if len(ks) == 0:
+                return
+            if on_pool:
+                xs = work.tile([P, POOL_GROUPS, D], BF16, name="xsp", tag="xsp")
+            else:
+                xs = work.tile([P, 4 - POOL_GROUPS, D], BF16, name="xsd", tag="xsd")
+            eng = nc.gpsimd if on_pool else nc.vector
+            for i, k in enumerate(ks):
+                xs_t[(u, k)] = xs[:, i, :]
+                eng.tensor_scalar(
+                    out=xs[:, i, :],
+                    in0=xr_t[u // 2][:, (u % 2) * 4 + k, :],
+                    scalar1=sq_t[u][:, k : k + 1],
+                    scalar2=mask_f[:, u * 4 + k : u * 4 + k + 1],
+                    op0=ALU.mult,
+                    op1=ALU.mult,
+                )
 
-        def scale_and_turn(c, h):
-            if not ok(c):
+        def turn(u):
+            if not ok(u):
                 return
-            xs = work.tile([P, 4, D], BF16, name="xs", tag="xs")
             for bank in range(2):
-                for gl in range(2):
-                    g = h * 4 + bank * 2 + gl
-                    nc.vector.tensor_scalar(
-                        out=xs[:, bank * 2 + gl, :],
-                        in0=xr_t[c][:, g, :],
-                        scalar1=sc_t[c][:, g : g + 1],
-                        scalar2=None,
-                        op0=ALU.mult,
-                    )
                 pt = ps_t.tile([P, 2, 2, P], F32, name="pt", tag="pt")
-                pt_t[(c, h, bank)] = pt
+                pt_t[(u, bank)] = pt
                 for gl in range(2):
-                    words = xs[:, bank * 2 + gl, :].bitcast(F32)
-                    for u in range(2):
-                        nc.tensor.transpose(out=pt[:, gl, u, :], in_=words[:, u * P : (u + 1) * P], identity=ident[:])
+                    words = xs_t[(u, bank * 2 + gl)].bitcast(F32)
+                    for w in range(2):
+                        nc.tensor.transpose(out=pt[:, gl, w, :], in_=words[:, w * P : (w + 1) * P], identity=ident[:])
 
-        def leave(u, bank, on_scalar):
-            c, h = unit(u)
+        def leave(u, bank):
+            if not ok(u):
+                return
             if bank == 0:
                 grp = work.tile([P, 2048], BF16, name="grp", tag="grp", align_bytes=64)
-                grp_t[(c, h)] = grp
-            src = pt_t[(c, h, bank)][:].rearrange("p j u r -> p j r u")
-            dst = grp_t[(c, h)][:, bank * 1024 : (bank + 1) * 1024].bitcast(F32).rearrange("p (j r u) -> p j r u", j=2, u=2)
-            if on_scalar:
+                grp_t[u] = grp
+            src = pt_t[(u, bank)][:].rearrange("p j w r -> p j r w")
+            dst = grp_t[u][:, bank * 1024 : (bank + 1) * 1024].bitcast(F32).rearrange("p (j r w) -> p j r w", j=2, w=2)
+            if bank < act_banks(u):
                 nc.scalar.copy(out=dst, in_=src)
             else:
                 nc.vector.tensor_copy(out=dst, in_=src)
 
-        def quantise(c, h):
-            if not ok(c):
+        def quantise(u):
+            if not ok(u):
                 return
-            if c < Q_CHUNKS:
-                lo = c * 1024 + h * 512
-                cod = a_cod[:, lo : lo + 512]
-                scl = a_scl[:, lo : lo + 512]
+            if u < 2 * Q_CHUNKS:
+                cod = a_cod[:, u * 512 : (u + 1) * 512]
+                scl = a_scl[:, u * 512 : (u + 1) * 512]
             else:
                 cod_tile = work.tile([P, 512], U32, name="cod_tile", tag="cod", align_bytes=64)
                 scl_tile = work.tile([P, 512], U8, name="scl_tile", tag="scl", align_bytes=64)
                 cod = cod_tile[:]
                 scl = scl_tile[:]
-                cod_t[(c, h)] = (cod, scl)
-            nc.vector.quantize_mx(out=cod.bitcast(FP8X4), scales=scl, in_=grp_t[(c, h)][:])
+                cod_t[u] = (cod, scl)
+            nc.vector.quantize_mx(out=cod.bitcast(FP8X4), scales=scl, in_=grp_t[u][:])
 
-        def multiply(c, h):
-            if not ok(c) or c < Q_CHUNKS:
+        def multiply(u):
+            if not ok(u) or u < 2 * Q_CHUNKS:
                 return
-            d = c - Q_CHUNKS
-            b = d // 2
-            cod, scl = cod_t[(c, h)]
+            b = (u // 2 - Q_CHUNKS) // 2
+            cod, scl = cod_t[u]
             for qt in range(2):
                 lo = b * 256 + qt * P
                 pm = ps_m.tile([P, 512], F32, name="pm", tag="pm")
-                pm_t[(c, h, qt)] = pm
+                pm_t[(u, qt)] = pm
                 nc.tensor.matmul_mx(
                     out=pm[:],
                     lhsT=a_cod[:, lo : lo + P].bitcast(FP8X4),
@@ -209,57 +217,39 @@ def tile_lateinteraction_t_kernel(tc, x1, x2, x1_mask, x2_mask, out):
                 )
 
         def best_of(u, qt):
-            c, h = unit(u)
-            if c < Q_CHUNKS:
+            if not ok(u) or u < 2 * Q_CHUNKS:
                 return
-            col = (c - Q_CHUNKS) * 4 + qt * 2 + h
-            nc.vector.tensor_reduce(
-                out=best[:, col : col + 1], in_=pm_t[(c, h, qt)][:], axis=AX.X, op=ALU.max
-            )
-
-        def unit(u):
-            return u // 2, u % 2
+            col = (u // 2 - Q_CHUNKS) * 4 + qt * 2 + u % 2
+            nc.vector.tensor_reduce(out=best[:, col : col + 1], in_=pm_t[(u, qt)][:], axis=AX.X, op=ALU.max)
 
         def act_banks(u):
             if u < 2 * Q_CHUNKS:
                 return 0
             if u >= UNITS - TAIL_UNITS:
                 return 2
-            return 1
+            return 1 if u % 4 != 3 else 0
 
         for c in range(LEAD):
             load(c)
         for s in range(UNITS + 6):
             if s % 2 == 0:
                 load(s // 2 + LEAD)
-            j = s // 2 - 1
-            chain = s % 2 == 0
-            if 0 <= s - 5 < UNITS:
-                quantise(*unit(s - 5))
-            if 0 <= s - 5 < UNITS:
-                multiply(*unit(s - 5))
-            if s < UNITS:
-                sumsq(s // 2, (s % 2) * 4, (s % 2) * 4 + 2)
-            if 0 <= s - 3 < UNITS:
-                scale_and_turn(*unit(s - 3))
-            if chain:
-                clamp(j)
-            if 0 <= s - 4 < UNITS:
-                leave(s - 4, 0, act_banks(s - 4) >= 1)
-            if chain:
-                root(j)
-            if 0 <= s - 4 < UNITS:
-                leave(s - 4, 1, act_banks(s - 4) >= 2)
-            if s < UNITS:
-                sumsq(s // 2, (s % 2) * 4 + 2, (s % 2) * 4 + 4)
-            if 0 <= s - 5 < UNITS:
-                best_of(s - 5, 0)
-            if chain:
-                invert(j)
-            if 0 <= s - 5 < UNITS:
-                best_of(s - 5, 1)
-            if chain:
-                factor(j)
+            if s == 4:
+                nc.gpsimd.tensor_copy(out=mask_f[:, QCOLS:], in_=mask_d[:])
+            quantise(s - 5)
+            multiply(s - 5)
+            scale(s - 3, False)
+            turn(s - 3)
+            invert(s - 2)
+            scale(s - 2, True)
+            sumsq(s, 0, 2)
+            leave(s - 4, 0)
+            root(s - 1)
+            sumsq(s, 2, 4)
+            leave(s - 4, 1)
+            clamp(s)
+            best_of(s - 5, 0)
+            best_of(s - 5, 1)
 
         both = const.tile([P, D_CHUNKS * 2], F32, name="both")
         nc.vector.tensor_reduce(

@@ -25,7 +25,7 @@ EPS2 = 1e-24
 UNITS = 2 * CHUNKS
 LEAD = 3
 TAIL_UNITS = 4
-POOL_GROUPS = 2
+POOL_GROUPS = 1
 
 
 def tile_lateinteraction_t_kernel(tc, x1, x2, x1_mask, x2_mask, out):
@@ -227,7 +227,7 @@ def tile_lateinteraction_t_kernel(tc, x1, x2, x1_mask, x2_mask, out):
                 return 0
             if u >= UNITS - TAIL_UNITS:
                 return 2
-            return 1 if u % 4 != 3 else 0
+            return 1 if u % 6 != 5 else 0
 
         for c in range(LEAD):
             load(c)

@@ -41,26 +41,31 @@ def tile_lateinteraction_t_kernel(tc, x1, x2, x1_mask, x2_mask, out):
         ps_m = ctx.enter_context(tc.psum_pool(name="ps_m", bufs=3))
         ps_q = ctx.enter_context(tc.psum_pool(name="ps_q", bufs=1))
 
+
+        QCOLS = Q_CHUNKS * GROUPS
+        rows_q = const.tile([P, 256], BF16, name="rows_q")
+        rows_d = const.tile([P, 1024], BF16, name="rows_d")
+        nc.vector.memset(rows_q[:], 0.0)
+        nc.scalar.dma_start(out=rows_q[0:16, :], in_=x1_mask)
+        nc.scalar.dma_start(out=rows_d[0:32, :], in_=x2_mask.rearrange("b n l -> (b n) l"))
+        nc.vector.memset(rows_d[32:64, :], 0.0)
+        nc.vector.memset(rows_d[64:128, :], 0.0)
+        ident_b = const.tile([P, P], BF16, name="ident_b")
+        make_identity(nc, ident_b[:])
+        ident = const.tile([P, P], F32, name="ident")
+        make_identity(nc, ident[:])
         warm = const.tile([P, 1], F32, name="warm")
         nc.vector.memset(warm[:], 1.0)
         nc.scalar.activation(out=warm[:], in_=warm[:], func=ACTF.Sqrt)
-
-        ident = const.tile([P, P], F32, name="ident")
-        make_identity(nc, ident[:])
-
-        QCOLS = Q_CHUNKS * GROUPS
-        mask_q = const.tile([P, QCOLS], BF16, name="mask_q")
-        mask_d = const.tile([P, D_CHUNKS * GROUPS], BF16, name="mask_d")
-        nc.scalar.dma_start(
-            out=mask_q[:].rearrange("p (b j) -> p b j", j=2),
-            in_=x1_mask.rearrange("b (p j) -> p b j", j=2),
-        )
-        nc.scalar.dma_start(
-            out=mask_d[:].rearrange("p (d j) -> p d j", j=GROUPS),
-            in_=x2_mask.rearrange("b n (p j) -> p (b n) j", j=GROUPS),
-        )
         mask_f = const.tile([P, CHUNKS * GROUPS], F32, name="mask_f")
-        nc.gpsimd.tensor_copy(out=mask_f[:, 0:QCOLS], in_=mask_q[:])
+        pmq = ps_q.tile([P, 2, P], BF16, name="pmq", tag="pq")
+        for j in range(2):
+            nc.tensor.transpose(out=pmq[:, j, :], in_=rows_q[:, j : 256 : 2], identity=ident_b[:])
+        nc.vector.tensor_copy(out=mask_f[:, 0:QCOLS].rearrange("p (b j) -> p j b", j=2), in_=pmq[:, :, 0:16])
+        pmd = ps_q.tile([P, GROUPS, P], BF16, name="pmd", tag="pq")
+        for j in range(GROUPS):
+            nc.tensor.transpose(out=pmd[:, j, :], in_=rows_d[:, j : 1024 : GROUPS], identity=ident_b[:])
+        nc.vector.tensor_copy(out=mask_f[:, QCOLS:].rearrange("p (d j) -> p j d", j=GROUPS), in_=pmd[:, :, 0:32])
 
         pick = const.tile([P, 4, P], F32, name="pick")
         nc.vector.memset(pick[:], 0.0)
@@ -234,8 +239,6 @@ def tile_lateinteraction_t_kernel(tc, x1, x2, x1_mask, x2_mask, out):
         for s in range(UNITS + 6):
             if s % 2 == 0:
                 load(s // 2 + LEAD)
-            if s == 4:
-                nc.gpsimd.tensor_copy(out=mask_f[:, QCOLS:], in_=mask_d[:])
             quantise(s - 5)
             multiply(s - 5)
             scale(s - 3, False)

@@ -38,8 +38,7 @@ def tile_lateinteraction_t_kernel(tc, x1, x2, x1_mask, x2_mask, out):
         small = ctx.enter_context(tc.tile_pool(name="small", bufs=4))
         work = ctx.enter_context(tc.tile_pool(name="work", bufs=3))
         ps_t = ctx.enter_context(tc.psum_pool(name="ps_t", bufs=4))
-        ps_m = ctx.enter_context(tc.psum_pool(name="ps_m", bufs=3))
-        ps_q = ctx.enter_context(tc.psum_pool(name="ps_q", bufs=1))
+        ps_m = ctx.enter_context(tc.psum_pool(name="ps_m", bufs=4))
 
 
         QCOLS = Q_CHUNKS * GROUPS
@@ -58,11 +57,11 @@ def tile_lateinteraction_t_kernel(tc, x1, x2, x1_mask, x2_mask, out):
         nc.vector.memset(warm[:], 1.0)
         nc.scalar.activation(out=warm[:], in_=warm[:], func=ACTF.Sqrt)
         mask_f = const.tile([P, CHUNKS * GROUPS], F32, name="mask_f")
-        pmq = ps_q.tile([P, 2, P], BF16, name="pmq", tag="pq")
+        pmq = ps_m.tile([P, 2, P], BF16, name="pmq", tag="pm")
         for j in range(2):
             nc.tensor.transpose(out=pmq[:, j, :], in_=rows_q[:, j : 256 : 2], identity=ident_b[:])
         nc.vector.tensor_copy(out=mask_f[:, 0:QCOLS].rearrange("p (b j) -> p j b", j=2), in_=pmq[:, :, 0:16])
-        pmd = ps_q.tile([P, GROUPS, P], BF16, name="pmd", tag="pq")
+        pmd = ps_m.tile([P, GROUPS, P], BF16, name="pmd", tag="pm")
         for j in range(GROUPS):
             nc.tensor.transpose(out=pmd[:, j, :], in_=rows_d[:, j : 1024 : GROUPS], identity=ident_b[:])
         nc.vector.tensor_copy(out=mask_f[:, QCOLS:].rearrange("p (d j) -> p j d", j=GROUPS), in_=pmd[:, :, 0:32])
@@ -236,7 +235,7 @@ def tile_lateinteraction_t_kernel(tc, x1, x2, x1_mask, x2_mask, out):
 
         for c in range(LEAD):
             load(c)
-        for s in range(UNITS + 6):
+        for s in range(UNITS + 7):
             if s % 2 == 0:
                 load(s // 2 + LEAD)
             quantise(s - 5)
@@ -251,8 +250,8 @@ def tile_lateinteraction_t_kernel(tc, x1, x2, x1_mask, x2_mask, out):
             sumsq(s, 2, 4)
             leave(s - 4, 1)
             clamp(s)
-            best_of(s - 5, 0)
-            best_of(s - 5, 1)
+            best_of(s - 6, 0)
+            best_of(s - 6, 1)
 
         both = const.tile([P, D_CHUNKS * 2], F32, name="both")
         nc.vector.tensor_reduce(
@@ -262,7 +261,7 @@ def tile_lateinteraction_t_kernel(tc, x1, x2, x1_mask, x2_mask, out):
         nc.vector.tensor_reduce(
             out=tot[:], in_=both[:].rearrange("p (d q) -> p d q", q=2), axis=AX.X, op=ALU.add
         )
-        pf = ps_q.tile([P, 8], F32, name="pf", tag="pq")
+        pf = ps_m.tile([P, 8], F32, name="pf", tag="pm")
         for i in range(4):
             nc.tensor.matmul(
                 out=pf[:], lhsT=pick[:, i, :], rhs=tot[:, i * 8 : (i + 1) * 8], start=(i == 0), stop=(i == 3)

@@ -231,7 +231,7 @@ def tile_lateinteraction_t_kernel(tc, x1, x2, x1_mask, x2_mask, out):
                 return 0
             if u >= UNITS - TAIL_UNITS:
                 return 2
-            return 1 if u % 6 != 5 else 0
+            return 1 if u % 12 != 11 else 0
 
         for c in range(LEAD):
             load(c)

from contextlib import ExitStack

import concourse.mybir as mybir
from concourse.masks import make_identity

FLOPS = 2 * 16 * 2 * 256 * 1024 * 512

BF16 = mybir.dt.bfloat16
F32 = mybir.dt.float32
U32 = mybir.dt.uint32
U8 = mybir.dt.uint8
FP8X4 = mybir.dt.float8_e4m3fn_x4
ALU = mybir.AluOpType
ACTF = mybir.ActivationFunctionType
AX = mybir.AxisListType

P = 128
D = 512
GROUPS = 8
Q_CHUNKS = 4
D_CHUNKS = 32
CHUNKS = Q_CHUNKS + D_CHUNKS
EPS2 = 1e-24

UNITS = 2 * CHUNKS
LEAD = 3
TAIL_UNITS = 4
POOL_GROUPS = 1


def tile_lateinteraction_t_kernel(tc, x1, x2, x1_mask, x2_mask, out):
    nc = tc.nc

    with ExitStack() as ctx:
        ctx.enter_context(tc.manual_schedule())
        const = ctx.enter_context(tc.tile_pool(name="const", bufs=1))
        xpool = ctx.enter_context(tc.tile_pool(name="xpool", bufs=6))
        small = ctx.enter_context(tc.tile_pool(name="small", bufs=4))
        work = ctx.enter_context(tc.tile_pool(name="work", bufs=3))
        ps_t = ctx.enter_context(tc.psum_pool(name="ps_t", bufs=4))
        ps_m = ctx.enter_context(tc.psum_pool(name="ps_m", bufs=4))


        QCOLS = Q_CHUNKS * GROUPS
        rows_q = const.tile([P, 256], BF16, name="rows_q")
        rows_d = const.tile([P, 1024], BF16, name="rows_d")
        nc.vector.memset(rows_q[:], 0.0)
        nc.scalar.dma_start(out=rows_q[0:16, :], in_=x1_mask)
        nc.scalar.dma_start(out=rows_d[0:32, :], in_=x2_mask.rearrange("b n l -> (b n) l"))
        nc.vector.memset(rows_d[32:64, :], 0.0)
        nc.vector.memset(rows_d[64:128, :], 0.0)
        ident_b = const.tile([P, P], BF16, name="ident_b")
        make_identity(nc, ident_b[:])
        ident = const.tile([P, P], F32, name="ident")
        make_identity(nc, ident[:])
        warm = const.tile([P, 1], F32, name="warm")
        nc.vector.memset(warm[:], 1.0)
        nc.scalar.activation(out=warm[:], in_=warm[:], func=ACTF.Sqrt)
        mask_f = const.tile([P, CHUNKS * GROUPS], F32, name="mask_f")
        pmq = ps_m.tile([P, 2, P], BF16, name="pmq", tag="pm")
        for j in range(2):
            nc.tensor.transpose(out=pmq[:, j, :], in_=rows_q[:, j : 256 : 2], identity=ident_b[:])
        nc.vector.tensor_copy(out=mask_f[:, 0:QCOLS].rearrange("p (b j) -> p j b", j=2), in_=pmq[:, :, 0:16])
        pmd = ps_m.tile([P, GROUPS, P], BF16, name="pmd", tag="pm")
        for j in range(GROUPS):
            nc.tensor.transpose(out=pmd[:, j, :], in_=rows_d[:, j : 1024 : GROUPS], identity=ident_b[:])
        nc.vector.tensor_copy(out=mask_f[:, QCOLS:].rearrange("p (d j) -> p j d", j=GROUPS), in_=pmd[:, :, 0:32])

        pick = const.tile([P, 4, P], F32, name="pick")
        nc.vector.memset(pick[:], 0.0)
        for i in range(4):
            nc.vector.memset(pick[:, i, i : i + 1], 1.0)

        junk = const.tile([P, 8, D], BF16, name="junk")
        a_cod = const.tile([P, Q_CHUNKS * 1024], U32, name="a_cod", align_bytes=64)
        a_scl = const.tile([P, Q_CHUNKS * 1024], U8, name="a_scl", align_bytes=64)
        best = const.tile([P, D_CHUNKS * 4], F32, name="best")

        xr_t = {}
        ss_t = {}
        sq_t = {}
        xs_t = {}
        pt_t = {}
        grp_t = {}
        cod_t = {}
        pm_t = {}

        def ok(u):
            return 0 <= u < UNITS

        def load(c):
            if not 0 <= c < CHUNKS:
                return
            xr = xpool.tile([P, GROUPS, D], BF16, name="xr", tag="xr")
            xr_t[c] = xr
            if c < Q_CHUNKS:
                pieces = 4 if c == 0 else (2 if c == 1 else 1)
                step = 4 // pieces
                for i in range(pieces):
                    nc.sync.dma_start(
                        out=xr[:, i * step * 2 : (i + 1) * step * 2, :].rearrange("p (b j) k -> p b (j k)", j=2),
                        in_=x1[c * 4 + i * step : c * 4 + (i + 1) * step].rearrange("b (p j) k -> p b (j k)", j=2),
                    )
            else:
                d = c - Q_CHUNKS
                nc.sync.dma_start(
                    out=xr[:].rearrange("p j k -> p (j k)"),
                    in_=x2[d // 2, d % 2].rearrange("(p j) k -> p (j k)", j=GROUPS),
                )

        def sumsq(u, k0, k1):
            if not ok(u):
                return
            if k0 == 0:
                ss = small.tile([P, 4], F32, name="ss", tag="ss")
                ss_t[u] = ss
            for k in range(k0, k1):
                g = (u % 2) * 4 + k
                nc.scalar.activation(
                    out=junk[:, g, :], in_=xr_t[u // 2][:, g, :], func=ACTF.Square, accum_out=ss_t[u][:, k : k + 1]
                )

        def clamp(u):
            if not ok(u):
                return
            cl = small.tile([P, 4], F32, name="cl", tag="cl")
            nc.gpsimd.tensor_scalar(out=cl[:], in0=ss_t[u][:], scalar1=EPS2, scalar2=0.0, op0=ALU.max, op1=ALU.add)
            sq_t[u] = cl

        def root(u):
            if not ok(u):
                return
            rt = small.tile([P, 4], F32, name="rt", tag="rt")
            nc.scalar.activation(out=rt[:], in_=sq_t[u][:], func=ACTF.Sqrt)
            sq_t[u] = rt

        def invert(u):
            if not ok(u):
                return
            rc = small.tile([P, 4], F32, name="rc", tag="rc")
            nc.vector.reciprocal(out=rc[:], in_=sq_t[u][:])
            sq_t[u] = rc

        def scale(u, on_pool):
            if not ok(u):
                return
            ks = range(0, POOL_GROUPS) if on_pool else range(POOL_GROUPS, 4)
            if len(ks) == 0:
                return
            if on_pool:
                xs = work.tile([P, POOL_GROUPS, D], BF16, name="xsp", tag="xsp")
            else:
                xs = work.tile([P, 4 - POOL_GROUPS, D], BF16, name="xsd", tag="xsd")
            eng = nc.gpsimd if on_pool else nc.vector
            for i, k in enumerate(ks):
                xs_t[(u, k)] = xs[:, i, :]
                eng.tensor_scalar(
                    out=xs[:, i, :],
                    in0=xr_t[u // 2][:, (u % 2) * 4 + k, :],
                    scalar1=sq_t[u][:, k : k + 1],
                    scalar2=mask_f[:, u * 4 + k : u * 4 + k + 1],
                    op0=ALU.mult,
                    op1=ALU.mult,
                )

        def turn(u):
            if not ok(u):
                return
            for bank in range(2):
                pt = ps_t.tile([P, 2, 2, P], F32, name="pt", tag="pt")
                pt_t[(u, bank)] = pt
                for gl in range(2):
                    words = xs_t[(u, bank * 2 + gl)].bitcast(F32)
                    for w in range(2):
                        nc.tensor.transpose(out=pt[:, gl, w, :], in_=words[:, w * P : (w + 1) * P], identity=ident[:])

        def leave(u, bank):
            if not ok(u):
                return
            if bank == 0:
                grp = work.tile([P, 2048], BF16, name="grp", tag="grp", align_bytes=64)
                grp_t[u] = grp
            src = pt_t[(u, bank)][:].rearrange("p j w r -> p j r w")
            dst = grp_t[u][:, bank * 1024 : (bank + 1) * 1024].bitcast(F32).rearrange("p (j r w) -> p j r w", j=2, w=2)
            if bank < act_banks(u):
                nc.scalar.copy(out=dst, in_=src)
            else:
                nc.vector.tensor_copy(out=dst, in_=src)

        def quantise(u):
            if not ok(u):
                return
            if u < 2 * Q_CHUNKS:
                cod = a_cod[:, u * 512 : (u + 1) * 512]
                scl = a_scl[:, u * 512 : (u + 1) * 512]
            else:
                cod_tile = work.tile([P, 512], U32, name="cod_tile", tag="cod", align_bytes=64)
                scl_tile = work.tile([P, 512], U8, name="scl_tile", tag="scl", align_bytes=64)
                cod = cod_tile[:]
                scl = scl_tile[:]
                cod_t[u] = (cod, scl)
            nc.vector.quantize_mx(out=cod.bitcast(FP8X4), scales=scl, in_=grp_t[u][:])

        def multiply(u):
            if not ok(u) or u < 2 * Q_CHUNKS:
                return
            b = (u // 2 - Q_CHUNKS) // 2
            cod, scl = cod_t[u]
            for qt in range(2):
                lo = b * 256 + qt * P
                pm = ps_m.tile([P, 512], F32, name="pm", tag="pm")
                pm_t[(u, qt)] = pm
                nc.tensor.matmul_mx(
                    out=pm[:],
                    lhsT=a_cod[:, lo : lo + P].bitcast(FP8X4),
                    lhsT_scale=a_scl[:, lo : lo + P],
                    rhs=cod.bitcast(FP8X4),
                    rhs_scale=scl,
                    start=True,
                    stop=True,
                )

        def best_of(u, qt):
            if not ok(u) or u < 2 * Q_CHUNKS:
                return
            col = (u // 2 - Q_CHUNKS) * 4 + qt * 2 + u % 2
            nc.vector.tensor_reduce(out=best[:, col : col + 1], in_=pm_t[(u, qt)][:], axis=AX.X, op=ALU.max)

        def act_banks(u):
            if u < 2 * Q_CHUNKS:
                return 0
            if u >= UNITS - TAIL_UNITS:
                return 2
            return 1 if u % 12 != 11 else 0

        for c in range(LEAD):
            load(c)
        for s in range(UNITS + 7):
            if s % 2 == 0:
                load(s // 2 + LEAD)
            quantise(s - 5)
            multiply(s - 5)
            scale(s - 3, False)
            turn(s - 3)
            invert(s - 2)
            scale(s - 2, True)
            sumsq(s, 0, 2)
            leave(s - 4, 0)
            root(s - 1)
            sumsq(s, 2, 4)
            leave(s - 4, 1)
            clamp(s)
            best_of(s - 6, 0)
            best_of(s - 6, 1)

        both = const.tile([P, D_CHUNKS * 2], F32, name="both")
        nc.vector.tensor_reduce(
            out=both[:], in_=best[:].rearrange("p (a h) -> p a h", h=2), axis=AX.X, op=ALU.max
        )
        tot = const.tile([P, D_CHUNKS], F32, name="tot")
        nc.vector.tensor_reduce(
            out=tot[:], in_=both[:].rearrange("p (d q) -> p d q", q=2), axis=AX.X, op=ALU.add
        )
        pf = ps_m.tile([P, 8], F32, name="pf", tag="pm")
        for i in range(4):
            nc.tensor.matmul(
                out=pf[:], lhsT=pick[:, i, :], rhs=tot[:, i * 8 : (i + 1) * 8], start=(i == 0), stop=(i == 3)
            )
        res = const.tile([P, 8], F32, name="res")
        nc.vector.tensor_copy(out=res[:], in_=pf[:])
        nc.sync.dma_start(out=out.rearrange("(i b) n -> i (b n)", i=4), in_=res[0:4, :])
